import numpy as np
import ml_dtypes


def mxq(x, axis, fmt="e4m3"):
    dtype, down = {"e4m3": (ml_dtypes.float8_e4m3fn, 7), "e5m2": (ml_dtypes.float8_e5m2, 14)}[fmt]
    v = np.moveaxis(np.asarray(x, np.float32).astype(ml_dtypes.bfloat16).astype(np.float64), axis, -1)
    blocks = v.reshape(v.shape[:-1] + (-1, 32))
    amax = np.abs(blocks).max(-1, keepdims=True)
    byte = np.maximum(np.where(amax > 0, np.frexp(amax)[1] - 1 + 127, 0) - down, 1)
    scale = np.exp2(byte - 127.0)
    codes = (blocks / scale).astype(np.float32).astype(dtype).astype(np.float64)
    return np.moveaxis((codes * scale).reshape(v.shape), -1, axis)


WIDE = False


def mx_kscale(k):
    if not WIDE:
        return np.ones(k)
    levels = np.array([10, -10, 5, -5, 0])
    a = np.random.permutation(np.resize(levels, k // 512 * 4)).reshape(k // 512, 4)
    idx = np.arange(k)
    return np.exp2(a[idx // 512, idx % 128 // 32])


BF16 = ml_dtypes.bfloat16


def bf(x):
    return np.asarray(x, np.float32).astype(BF16)


def f64(x):
    return np.asarray(x).astype(np.float64)


B, L0, L1, L2, L3 = 2048, 256, 512, 512, 256
NA = 5


def _act(x, a):
    return a[:, 0] * np.tanh(x) * np.sin(a[:, 1] * x + a[:, 2]) + a[:, 3] * x + a[:, 4]


def _gain(t):
    one = np.ones_like(t)
    return np.stack([t, one, one, t, t], axis=1)


def setup_inputs():
    t, u = mx_kscale(L1), mx_kscale(L2)
    return {"data": bf(np.random.standard_normal((B, L0))),
            "W1": bf(np.random.standard_normal((L0, L1)) * 1.0 / np.sqrt(L0)),
            "b1": bf(np.random.standard_normal(L1) * 0.1),
            "a1": bf(np.random.random((L1, NA)) * _gain(t)),
            "W2": bf(np.random.standard_normal((L1, L2)) * 1.2 / np.sqrt(L1) / t[:, None]),
            "b2": bf(np.random.standard_normal(L2) * 0.1),
            "a2": bf(np.random.random((L2, NA)) * _gain(u)),
            "W3": bf(np.random.standard_normal((L2, L3)) * 2.0 / np.sqrt(L2) / u[:, None]),
            "b3": bf(np.random.standard_normal(L3) * 0.1),
            "a3": bf(np.random.random((L3, NA)))}


def reference(data, W1, b1, a1, W2, b2, a2, W3, b3, a3):
    h = _act(f64(data) @ f64(W1) + f64(b1), f64(a1))
    h = _act((mxq(h, 1, "e4m3") @ mxq(f64(W2), 0, "e4m3")) + f64(b2), f64(a2))
    h = _act((mxq(h, 1, "e4m3") @ mxq(f64(W3), 0, "e4m3")) + f64(b3), f64(a3))
    e = np.exp(h - h.max(axis=1, keepdims=True))
    return e / e.sum(axis=1, keepdims=True)

@@ -1,0 +1,310 @@
+from contextlib import ExitStack
+import math
+
+import concourse.mybir as mybir
+from concourse.masks import make_identity
+
+FLOPS = 2 * 2048 * (256 * 512 + 512 * 512 + 512 * 256)
+
+F32 = mybir.dt.float32
+BF16 = mybir.dt.bfloat16
+I32 = mybir.dt.int32
+U32 = mybir.dt.uint32
+U8 = mybir.dt.uint8
+FP8X4 = mybir.dt.float8_e4m3fn_x4
+ACT = mybir.ActivationFunctionType
+ALU = mybir.AluOpType
+AX = mybir.AxisListType
+
+P = 128
+CW = 512
+NCH = 4
+TWO_PI = 2.0 * math.pi
+INV_2PI = 1.0 / (2.0 * math.pi)
+
+MANUAL = True
+
+
+def tile_network_kernel(tc, data, W1, b1, a1, W2, b2, a2, W3, b3, a3, out):
+    nc = tc.nc
+    with ExitStack() as ctx:
+        const = ctx.enter_context(tc.tile_pool(name="const", bufs=1))
+        work = ctx.enter_context(tc.tile_pool(name="work", bufs=2))
+        psum = ctx.enter_context(tc.psum_pool(name="psum", bufs=8))
+        if MANUAL:
+            ctx.enter_context(tc.manual_schedule())
+
+        a1r = const.tile([P, 4, 5], BF16, name="a1r")
+        b1r = const.tile([P, 4], BF16, name="b1r")
+        a2r = const.tile([P, 4, 5], BF16, name="a2r")
+        b2r = const.tile([P, 4], BF16, name="b2r")
+        a3r = const.tile([P, 2, 5], BF16, name="a3r")
+        b3r = const.tile([P, 2], BF16, name="b3r")
+        data_sb = const.tile([P, 16, 256], BF16, name="data_sb")
+        w1r = const.tile([P, 2, 512], BF16, name="w1r")
+        w2r = const.tile([P, 4, 512], BF16, name="w2r")
+        w3r = const.tile([P, 4, 256], BF16, name="w3r")
+        dview = data.rearrange("(p n) k -> p n k", n=16)
+        oview = out.rearrange("(p n) c -> p n c", n=16)
+
+        nc.sync.dma_start(out=a1r[:], in_=a1.rearrange("(p t) c -> p t c", t=4))
+        nc.sync.dma_start(out=b1r[:], in_=b1.rearrange("(p t) -> p t", t=4))
+        nc.sync.dma_start(out=data_sb[:, 0:4, :], in_=dview[:, 0:4, :])
+        nc.sync.dma_start(out=w1r[:], in_=W1.rearrange("(kt q) n -> q kt n", q=P))
+        nc.sync.dma_start(out=w2r[:], in_=W2.rearrange("(p j) n -> p j n", j=4))
+        nc.sync.dma_start(out=w3r[:], in_=W3.rearrange("(p j) n -> p j n", j=4))
+        nc.sync.dma_start(out=data_sb[:, 4:16, :], in_=dview[:, 4:16, :])
+
+        warm = const.tile([P, 1], F32, name="warm")
+        nc.vector.memset(warm[:], 0.0)
+        nc.scalar.activation(out=warm[:], in_=warm[:], func=ACT.Silu)
+
+        nc.scalar.dma_start(out=a2r[:], in_=a2.rearrange("(p t) c -> p t c", t=4))
+        nc.scalar.dma_start(out=b2r[:], in_=b2.rearrange("(p t) -> p t", t=4))
+        nc.scalar.dma_start(out=a3r[:], in_=a3.rearrange("(t p) c -> p t c", p=P))
+        with nc.allow_non_contiguous_dma(reason="256 bias values, one per partition and node tile"):
+            nc.scalar.dma_start(out=b3r[:], in_=b3.rearrange("(t p) -> p t", p=P))
+
+        identb = const.tile([P, P], BF16, name="identb")
+        make_identity(nc, identb[:])
+        identf = const.tile([P, P], F32, name="identf")
+        make_identity(nc, identf[:])
+
+        w1p = const.tile([P, 2, 4, P], BF16, name="w1p")
+        w1v = w1r.rearrange("q kt (m t) -> q kt t m", t=4)
+        for t in range(4):
+            nc.vector.tensor_copy(out=w1p[:, :, t, :], in_=w1v[:, :, t, :])
+
+        prm = const.tile([P, 6, 10], F32, name="prm")
+        a32s = []
+
+        def prep(ar, br, nt, s0):
+            sl = slice(s0, s0 + nt)
+            a32 = const.tile([P, nt, 5], F32, name="a32_%d" % s0)
+            a32s.append(a32)
+            nc.vector.tensor_copy(out=a32[:], in_=ar[:])
+            nc.vector.tensor_copy(out=prm[:, 0, sl], in_=br[:])
+            nc.vector.tensor_tensor(out=prm[:, 3, sl], in0=a32[:, :, 1], in1=prm[:, 0, sl], op=ALU.mult)
+            nc.vector.tensor_tensor(out=prm[:, 3, sl], in0=prm[:, 3, sl], in1=a32[:, :, 2], op=ALU.add)
+            nc.vector.tensor_scalar(out=prm[:, 2, sl], in0=prm[:, 3, sl], scalar1=INV_2PI, scalar2=None, op0=ALU.mult)
+            nc.vector.tensor_scalar(out=prm[:, 1, sl], in0=a32[:, :, 1], scalar1=INV_2PI, scalar2=None, op0=ALU.mult)
+            nc.vector.tensor_tensor(out=prm[:, 5, sl], in0=a32[:, :, 3], in1=prm[:, 0, sl], op=ALU.mult)
+            nc.vector.tensor_tensor(out=prm[:, 5, sl], in0=prm[:, 5, sl], in1=a32[:, :, 4], op=ALU.add)
+
+        prep(a1r, b1r, 4, 0)
+        prep(a2r, b2r, 4, 4)
+        prep(a3r, b3r, 2, 8)
+
+        g2 = const.tile([P, 512, 4], BF16, name="g2", align_bytes=64)
+        nc.gpsimd.tensor_scalar(
+            out=g2.rearrange("p (t m) j -> p t m j", t=4),
+            in0=w2r.rearrange("p j (m t) -> p t m j", t=4),
+            scalar1=1.0, scalar2=0.0, op0=ALU.mult, op1=ALU.add,
+        )
+        g3 = const.tile([P, 256, 4], BF16, name="g3", align_bytes=64)
+        nc.gpsimd.tensor_scalar(
+            out=g3[:], in0=w3r.rearrange("p j n -> p n j"),
+            scalar1=1.0, scalar2=0.0, op0=ALU.mult, op1=ALU.add,
+        )
+        w2c = const.tile([P, 512], U32, name="w2c", align_bytes=64)
+        w2s = const.tile([P, 512], U8, name="w2s", align_bytes=64)
+        w3c = const.tile([P, 256], U32, name="w3c", align_bytes=64)
+        w3s = const.tile([P, 256], U8, name="w3s", align_bytes=64)
+
+        hc = [const.tile([P, NCH, CW], U32, name="hc%d" % l, align_bytes=64) for l in range(2)]
+        hs = [const.tile([P, NCH, CW], U8, name="hs%d" % l, align_bytes=64) for l in range(2)]
+        h3 = const.tile([P, NCH, 2, CW], F32, name="h3")
+        dT = [const.tile([P, 2, CW], BF16, name="dT%d" % c) for c in range(NCH)]
+        ex = const.tile([P, 16, 256], F32, name="ex")
+        nmx = const.tile([P, 16], F32, name="nmx")
+        ssum = const.tile([P, 16], F32, name="ssum")
+        rs = const.tile([P, 16], F32, name="rs")
+
+        units = []
+        for c in range(NCH):
+            for t in range(4):
+                units.append((0, c, t))
+        for c in range(NCH):
+            for t in range(4):
+                units.append((1, c, t))
+        for c in range(NCH):
+            for t in range(2):
+                units.append((2, c, t))
+        NU = len(units)
+        st = {}
+
+        def slot(u):
+            l, c, t = units[u]
+            return 4 * l + t
+
+        def par(row, u):
+            s = slot(u)
+            return prm[:, row, s:s + 1]
+
+        def apar(col, u):
+            l, c, t = units[u]
+            return a32s[l][:, t, col:col + 1]
+
+        def data_transposes(c):
+            tp = psum.tile([P, 2, CW], BF16, name="tp", tag="bank")
+            for kt in range(2):
+                for nl in range(4):
+                    nc.tensor.transpose(
+                        tp[:, kt, nl * P:(nl + 1) * P],
+                        data_sb[:, 4 * c + nl, kt * P:(kt + 1) * P],
+                        identb[:],
+                    )
+            st["tp", c] = tp
+
+        def data_evac(c):
+            nc.scalar.copy(out=dT[c][:], in_=st["tp", c][:])
+
+        def pe(u):
+            l, c, t = units[u]
+            z = psum.tile([P, CW], F32, name="z", tag="bank")
+            st["z", u] = z
+            if l == 0:
+                for kt in range(2):
+                    nc.tensor.matmul(out=z[:], lhsT=w1p[:, kt, t, :], rhs=dT[c][:, kt, :],
+                                     start=(kt == 0), stop=(kt == 1))
+            else:
+                wc, ws = (w2c, w2s) if l == 1 else (w3c, w3s)
+                nc.tensor.matmul_mx(
+                    out=z[:],
+                    lhsT=wc[:, t * P:(t + 1) * P].bitcast(FP8X4),
+                    lhsT_scale=ws[:, t * P:(t + 1) * P],
+                    rhs=hc[l - 1][:, c, :].bitcast(FP8X4),
+                    rhs_scale=hs[l - 1][:, c, :],
+                    start=True, stop=True,
+                )
+
+        def tanh(u):
+            tt = work.tile([P, CW], F32, name="tt", tag="tt", bufs=6)
+            st["t", u] = tt
+            nc.scalar.activation(out=tt[:], in_=st["z", u][:], func=ACT.Tanh, bias=par(0, u), scale=1.0)
+
+        def reduce_arg(u):
+            z = st["z", u]
+            nn = work.tile([P, CW], I32, name="nn", tag="nn", bufs=2)
+            ff = work.tile([P, CW], F32, name="ff", tag="ff", bufs=4)
+            st["f", u] = ff
+            nc.vector.tensor_scalar(out=nn[:], in0=z[:], scalar1=par(1, u), scalar2=par(2, u),
+                                    op0=ALU.mult, op1=ALU.add)
+            nc.vector.scalar_tensor_tensor(out=ff[:], in0=z[:], scalar=par(1, u), in1=nn[:],
+                                           op0=ALU.mult, op1=ALU.subtract)
+
+        def sin(u):
+            ff = st["f", u]
+            nc.scalar.activation(out=ff[:], in_=ff[:], func=ACT.Sin, bias=par(3, u), scale=TWO_PI)
+
+        def prod(u):
+            tt = st["t", u]
+            nc.gpsimd.tensor_tensor(out=tt[:], in0=tt[:], in1=st["f", u][:], op=ALU.mult)
+
+        def affine(u):
+            tt = st["t", u]
+            nc.scalar.activation(out=tt[:], in_=tt[:], func=ACT.Identity, bias=par(5, u), scale=apar(0, u))
+
+        def combine(u):
+            l, c, t = units[u]
+            if l < 2:
+                if t == 0:
+                    st["h", l, c] = work.tile([P, 4, CW], BF16, name="hh", tag="hh", bufs=2)
+                dst = st["h", l, c][:, t, :]
+            else:
+                dst = h3[:, c, t, :]
+            nc.vector.scalar_tensor_tensor(out=dst, in0=st["z", u][:], scalar=apar(3, u), in1=st["t", u][:],
+                                           op0=ALU.mult, op1=ALU.add)
+
+        def regroup(l, c):
+            gg = work.tile([P, CW, 4], BF16, name="gg", tag="gg", bufs=2, align_bytes=64)
+            st["g", l, c] = gg
+            nc.vector.tensor_copy(
+                out=gg.rearrange("p (c i) t -> p c t i", i=4),
+                in_=st["h", l, c].rearrange("p t (c i) -> p c t i", i=4),
+            )
+
+        def quantise(l, c):
+            nc.vector.quantize_mx(
+                out=hc[l][:, c, :].bitcast(FP8X4),
+                scales=hs[l][:, c, :],
+                in_=st["g", l, c].rearrange("p w t -> p (w t)"),
+            )
+
+        def out_transposes(c):
+            for half in range(2):
+                ot = psum.tile([P, 2, 256], F32, name="ot", tag="bank")
+                st["o", c, half] = ot
+                for j in range(2):
+                    nl = 2 * half + j
+                    for t in range(2):
+                        nc.tensor.transpose(ot[:, j, t * P:(t + 1) * P], h3[:, c, t, nl * P:(nl + 1) * P], identf[:])
+
+        def row_max(c):
+            for half in range(2):
+                n0 = 4 * c + 2 * half
+                nc.vector.tensor_reduce(out=nmx[:, n0:n0 + 2], in_=st["o", c, half][:], axis=AX.X, op=ALU.max,
+                                        negate=True)
+
+        def exps(c):
+            for half in range(2):
+                for j in range(2):
+                    n = 4 * c + 2 * half + j
+                    nc.scalar.activation(out=ex[:, n, :], in_=st["o", c, half][:, j, :], func=ACT.Exp,
+                                         bias=nmx[:, n:n + 1], scale=1.0, accum_out=ssum[:, n:n + 1])
+
+        def normalise(c):
+            nc.vector.reciprocal(out=rs[:, 4 * c:4 * c + 4], in_=ssum[:, 4 * c:4 * c + 4])
+            for n in range(4 * c, 4 * c + 4):
+                nc.vector.tensor_scalar(out=ex[:, n, :], in0=ex[:, n, :], scalar1=rs[:, n:n + 1], scalar2=None,
+                                        op0=ALU.mult)
+            nc.sync.dma_start(out=oview[:, 4 * c:4 * c + 4, :], in_=ex[:, 4 * c:4 * c + 4, :])
+
+        data_transposes(0)
+        data_evac(0)
+        pending_quant = []
+        for k in range(-1, NU + 5):
+            for c in range(1, NCH):
+                if k == 4 * c - 3:
+                    data_transposes(c)
+            if 0 <= k + 1 < NU:
+                pe(k + 1)
+            for c in range(NCH):
+                if k == 38 + 2 * c:
+                    out_transposes(c)
+            if 0 <= k < NU:
+                tanh(k)
+            if 0 <= k - 4 < NU:
+                combine(k - 4)
+            for (l, c) in pending_quant:
+                quantise(l, c)
+            pending_quant = []
+            if 0 <= k - 4 < NU:
+                l, c, t = units[k - 4]
+                if l < 2 and t == 3:
+                    regroup(l, c)
+                    pending_quant.append((l, c))
+            if k == 5:
+                nc.vector.quantize_mx(out=w2c[:].bitcast(FP8X4), scales=w2s[:],
+                                      in_=g2.rearrange("p w j -> p (w j)"))
+            if k == 7:
+                nc.vector.quantize_mx(out=w3c[:].bitcast(FP8X4), scales=w3s[:],
+                                      in_=g3.rearrange("p w j -> p (w j)"))
+            if 0 <= k < NU:
+                reduce_arg(k)
+            for c in range(NCH):
+                if k == 38 + 2 * c:
+                    row_max(c)
+            if 0 <= k - 1 < NU:
+                sin(k - 1)
+            if 0 <= k - 2 < NU:
+                prod(k - 2)
+            if 0 <= k - 3 < NU:
+                affine(k - 3)
+            for c in range(1, NCH):
+                if k == 4 * c - 2:
+                    data_evac(c)
+
+        for c in range(NCH):
+            exps(c)
+            normalise(c)

@@ -23,6 +23,12 @@ TWO_PI = 2.0 * math.pi
 INV_2PI = 1.0 / (2.0 * math.pi)
 
 MANUAL = True
+PE_A = 2
+T_A = 1
+LS, LP, LQ, LH = 1, 2, 3, 4
+POOL_Q_MOD = 0
+REG_ACT = ()
+REG_PIECES = 2
 
 
 def tile_network_kernel(tc, data, W1, b1, a1, W2, b2, a2, W3, b3, a3, out):
@@ -132,13 +138,11 @@ def tile_network_kernel(tc, data, W1, b1, a1, W2, b2, a2, W3, b3, a3, out):
                 units.append((2, c, t))
         NU = len(units)
         st = {}
-
-        def slot(u):
-            l, c, t = units[u]
-            return 4 * l + t
+        live = [0]
 
         def par(row, u):
-            s = slot(u)
+            l, c, t = units[u]
+            s = 4 * l + t
             return prm[:, row, s:s + 1]
 
         def apar(col, u):
@@ -147,6 +151,7 @@ def tile_network_kernel(tc, data, W1, b1, a1, W2, b2, a2, W3, b3, a3, out):
 
         def data_transposes(c):
             tp = psum.tile([P, 2, CW], BF16, name="tp", tag="bank")
+            live[0] += 1
             for kt in range(2):
                 for nl in range(4):
                     nc.tensor.transpose(
@@ -158,11 +163,13 @@ def tile_network_kernel(tc, data, W1, b1, a1, W2, b2, a2, W3, b3, a3, out):
 
         def data_evac(c):
             nc.scalar.copy(out=dT[c][:], in_=st["tp", c][:])
+            live[0] -= 1
 
         def pe(u):
             l, c, t = units[u]
             z = psum.tile([P, CW], F32, name="z", tag="bank")
             st["z", u] = z
+            live[0] += 1
             if l == 0:
                 for kt in range(2):
                     nc.tensor.matmul(out=z[:], lhsT=w1p[:, kt, t, :], rhs=dT[c][:, kt, :],
@@ -179,18 +186,20 @@ def tile_network_kernel(tc, data, W1, b1, a1, W2, b2, a2, W3, b3, a3, out):
                 )
 
         def tanh(u):
-            tt = work.tile([P, CW], F32, name="tt", tag="tt", bufs=6)
+            tt = work.tile([P, CW], F32, name="tt", tag="tt", bufs=8)
             st["t", u] = tt
             nc.scalar.activation(out=tt[:], in_=st["z", u][:], func=ACT.Tanh, bias=par(0, u), scale=1.0)
 
-        def reduce_arg(u):
-            z = st["z", u]
+        def round_arg(u):
             nn = work.tile([P, CW], I32, name="nn", tag="nn", bufs=2)
+            st["n", u] = nn
+            nc.vector.tensor_scalar(out=nn[:], in0=st["z", u][:], scalar1=par(1, u), scalar2=par(2, u),
+                                    op0=ALU.mult, op1=ALU.add)
+
+        def frac_arg(u):
             ff = work.tile([P, CW], F32, name="ff", tag="ff", bufs=4)
             st["f", u] = ff
-            nc.vector.tensor_scalar(out=nn[:], in0=z[:], scalar1=par(1, u), scalar2=par(2, u),
-                                    op0=ALU.mult, op1=ALU.add)
-            nc.vector.scalar_tensor_tensor(out=ff[:], in0=z[:], scalar=par(1, u), in1=nn[:],
+            nc.vector.scalar_tensor_tensor(out=ff[:], in0=st["z", u][:], scalar=par(1, u), in1=st["n", u][:],
                                            op0=ALU.mult, op1=ALU.subtract)
 
         def sin(u):
@@ -201,28 +210,39 @@ def tile_network_kernel(tc, data, W1, b1, a1, W2, b2, a2, W3, b3, a3, out):
             tt = st["t", u]
             nc.gpsimd.tensor_tensor(out=tt[:], in0=tt[:], in1=st["f", u][:], op=ALU.mult)
 
+        def pool_q(u):
+            return u >= NU - 4 or (u % 4) < POOL_Q_MOD
+
         def affine(u):
             tt = st["t", u]
-            nc.scalar.activation(out=tt[:], in_=tt[:], func=ACT.Identity, bias=par(5, u), scale=apar(0, u))
+            if pool_q(u):
+                nc.gpsimd.tensor_scalar(out=tt[:], in0=tt[:], scalar1=apar(0, u), scalar2=par(5, u),
+                                        op0=ALU.mult, op1=ALU.add)
+            else:
+                nc.scalar.activation(out=tt[:], in_=tt[:], func=ACT.Identity, bias=par(5, u), scale=apar(0, u))
 
         def combine(u):
             l, c, t = units[u]
             if l < 2:
                 if t == 0:
-                    st["h", l, c] = work.tile([P, 4, CW], BF16, name="hh", tag="hh", bufs=2)
+                    st["h", l, c] = work.tile([P, 4, CW], BF16, name="hh", tag="hh", bufs=3)
                 dst = st["h", l, c][:, t, :]
             else:
                 dst = h3[:, c, t, :]
             nc.vector.scalar_tensor_tensor(out=dst, in0=st["z", u][:], scalar=apar(3, u), in1=st["t", u][:],
                                            op0=ALU.mult, op1=ALU.add)
+            live[0] -= 1
 
-        def regroup(l, c):
-            gg = work.tile([P, CW, 4], BF16, name="gg", tag="gg", bufs=2, align_bytes=64)
-            st["g", l, c] = gg
-            nc.vector.tensor_copy(
-                out=gg.rearrange("p (c i) t -> p c t i", i=4),
-                in_=st["h", l, c].rearrange("p t (c i) -> p c t i", i=4),
-            )
+        def regroup(l, c, piece, pieces):
+            if piece == 0:
+                st["g", l, c] = work.tile([P, CW, 4], BF16, name="gg", tag="gg", bufs=3, align_bytes=64)
+            w = CW // pieces
+            dst = st["g", l, c][:, piece * w:(piece + 1) * w, :].rearrange("p (c i) t -> p c t i", i=4)
+            src = st["h", l, c][:, :, piece * w:(piece + 1) * w].rearrange("p t (c i) -> p c t i", i=4)
+            if (l, c) in REG_ACT:
+                nc.scalar.copy(out=dst, in_=src)
+            else:
+                nc.vector.tensor_copy(out=dst, in_=src)
 
         def quantise(l, c):
             nc.vector.quantize_mx(
@@ -235,6 +255,7 @@ def tile_network_kernel(tc, data, W1, b1, a1, W2, b2, a2, W3, b3, a3, out):
             for half in range(2):
                 ot = psum.tile([P, 2, 256], F32, name="ot", tag="bank")
                 st["o", c, half] = ot
+                live[0] += 1
                 for j in range(2):
                     nl = 2 * half + j
                     for t in range(2):
@@ -252,6 +273,7 @@ def tile_network_kernel(tc, data, W1, b1, a1, W2, b2, a2, W3, b3, a3, out):
                     n = 4 * c + 2 * half + j
                     nc.scalar.activation(out=ex[:, n, :], in_=st["o", c, half][:, j, :], func=ACT.Exp,
                                          bias=nmx[:, n:n + 1], scale=1.0, accum_out=ssum[:, n:n + 1])
+                live[0] -= 1
 
         def normalise(c):
             nc.vector.reciprocal(out=rs[:, 4 * c:4 * c + 4], in_=ssum[:, 4 * c:4 * c + 4])
@@ -262,28 +284,25 @@ def tile_network_kernel(tc, data, W1, b1, a1, W2, b2, a2, W3, b3, a3, out):
 
         data_transposes(0)
         data_evac(0)
-        pending_quant = []
-        for k in range(-1, NU + 5):
-            for c in range(1, NCH):
-                if k == 4 * c - 3:
-                    data_transposes(c)
-            if 0 <= k + 1 < NU:
-                pe(k + 1)
-            for c in range(NCH):
-                if k == 38 + 2 * c:
-                    out_transposes(c)
+        quant_q = []
+        reg_q = []
+        otr_q = []
+        max_q = []
+        exp_q = []
+        for k in range(-PE_A, NU + LH):
+            if 0 <= k + T_A < NU:
+                tanh(k + T_A)
+            if 0 <= k - LS < NU:
+                sin(k - LS)
             if 0 <= k < NU:
-                tanh(k)
-            if 0 <= k - 4 < NU:
-                combine(k - 4)
-            for (l, c) in pending_quant:
-                quantise(l, c)
-            pending_quant = []
-            if 0 <= k - 4 < NU:
-                l, c, t = units[k - 4]
-                if l < 2 and t == 3:
-                    regroup(l, c)
-                    pending_quant.append((l, c))
+                round_arg(k)
+            j = k - LH
+            if 0 <= j < NU:
+                combine(j)
+            for q in quant_q:
+                if q[0] <= k:
+                    quantise(q[1], q[2])
+            quant_q = [q for q in quant_q if q[0] > k]
             if k == 5:
                 nc.vector.quantize_mx(out=w2c[:].bitcast(FP8X4), scales=w2s[:],
                                       in_=g2.rearrange("p w j -> p (w j)"))
@@ -291,20 +310,54 @@ def tile_network_kernel(tc, data, W1, b1, a1, W2, b2, a2, W3, b3, a3, out):
                 nc.vector.quantize_mx(out=w3c[:].bitcast(FP8X4), scales=w3s[:],
                                       in_=g3.rearrange("p w j -> p (w j)"))
             if 0 <= k < NU:
-                reduce_arg(k)
-            for c in range(NCH):
-                if k == 38 + 2 * c:
-                    row_max(c)
-            if 0 <= k - 1 < NU:
-                sin(k - 1)
-            if 0 <= k - 2 < NU:
-                prod(k - 2)
-            if 0 <= k - 3 < NU:
-                affine(k - 3)
+                frac_arg(k)
+            if 0 <= j < NU:
+                l, c, t = units[j]
+                if l < 2 and t == 3:
+                    if (l, c) in REG_ACT:
+                        for piece in range(REG_PIECES):
+                            reg_q.append((k + piece, l, c, piece))
+                        quant_q.append((k + REG_PIECES + 1, l, c))
+                    else:
+                        regroup(l, c, 0, 1)
+                        quant_q.append((k + 1, l, c))
+                if l == 2 and t == 1:
+                    otr_q.append(c)
+            if 0 <= k - LP < NU:
+                prod(k - LP)
+                if pool_q(k - LP):
+                    affine(k - LP)
+            if 0 <= k - LQ < NU and not pool_q(k - LQ):
+                affine(k - LQ)
+            for q in reg_q:
+                if q[0] <= k:
+                    regroup(q[1], q[2], q[3], REG_PIECES)
+            reg_q = [q for q in reg_q if q[0] > k]
             for c in range(1, NCH):
-                if k == 4 * c - 2:
+                if k == 4 * c - PE_A:
                     data_evac(c)
+            for c in range(1, NCH):
+                if k == 4 * c - PE_A - 1:
+                    data_transposes(c)
+            if 0 <= k + PE_A < NU:
+                pe(k + PE_A)
+            if len(otr_q) > 0 and live[0] <= 6 and k < NU + LH - 1:
+                out_transposes(otr_q[0])
+                max_q.append(otr_q[0])
+                otr_q = otr_q[1:]
+            if k >= NU - 1 and len(max_q) > 0:
+                row_max(max_q[0])
+                exp_q.append(max_q[0])
+                max_q = max_q[1:]
+            if k - LS >= NU - 1:
+                for c in exp_q:
+                    exps(c)
+                exp_q = []
 
-        for c in range(NCH):
-            exps(c)
-            normalise(c)
+        normalise(0)
+        out_transposes(3)
+        row_max(3)
+        exps(3)
+        normalise(1)
+        normalise(2)
+        normalise(3)

@@ -26,8 +26,8 @@ MANUAL = True
 PE_A = 2
 T_A = 1
 LS, LP, LQ, LH = 1, 2, 3, 4
-POOL_Q_MOD = 0
-REG_ACT = ()
+POOL_Q_MOD = 2
+REG_ACT = ((0, 0), (0, 1), (0, 2), (0, 3), (1, 0), (1, 1), (1, 2))
 REG_PIECES = 2
 
 

@@ -22,9 +22,10 @@ NCH = 4
 TWO_PI = 2.0 * math.pi
 INV_2PI = 1.0 / (2.0 * math.pi)
 
-MANUAL = True
+MANUAL = False
 PE_A = 2
 T_A = 1
+DVE_COLS = 128
 LS, LP, LQ, LH = 1, 2, 3, 4
 POOL_Q_MOD = 2
 REG_ACT = ((0, 0), (0, 1), (0, 2), (0, 3), (1, 0), (1, 1), (1, 2))
@@ -233,13 +234,12 @@ def tile_network_kernel(tc, data, W1, b1, a1, W2, b2, a2, W3, b3, a3, out):
                                            op0=ALU.mult, op1=ALU.add)
             live[0] -= 1
 
-        def regroup(l, c, piece, pieces):
-            if piece == 0:
+        def regroup(l, c, w0, w1, on_scalar):
+            if w0 == 0:
                 st["g", l, c] = work.tile([P, CW, 4], BF16, name="gg", tag="gg", bufs=3, align_bytes=64)
-            w = CW // pieces
-            dst = st["g", l, c][:, piece * w:(piece + 1) * w, :].rearrange("p (c i) t -> p c t i", i=4)
-            src = st["h", l, c][:, :, piece * w:(piece + 1) * w].rearrange("p t (c i) -> p c t i", i=4)
-            if (l, c) in REG_ACT:
+            dst = st["g", l, c][:, w0:w1, :].rearrange("p (c i) t -> p c t i", i=4)
+            src = st["h", l, c][:, :, w0:w1].rearrange("p t (c i) -> p c t i", i=4)
+            if on_scalar:
                 nc.scalar.copy(out=dst, in_=src)
             else:
                 nc.vector.tensor_copy(out=dst, in_=src)
@@ -253,13 +253,12 @@ def tile_network_kernel(tc, data, W1, b1, a1, W2, b2, a2, W3, b3, a3, out):
 
         def out_transposes(c):
             for half in range(2):
-                ot = psum.tile([P, 2, 256], F32, name="ot", tag="bank")
-                st["o", c, half] = ot
+                st["o", c, half] = psum.tile([P, 2, 256], F32, name="ot", tag="bank")
                 live[0] += 1
-                for j in range(2):
-                    nl = 2 * half + j
-                    for t in range(2):
-                        nc.tensor.transpose(ot[:, j, t * P:(t + 1) * P], h3[:, c, t, nl * P:(nl + 1) * P], identf[:])
+            for t in range(2):
+                for nl in range(4):
+                    nc.tensor.transpose(st["o", c, nl // 2][:, nl % 2, t * P:(t + 1) * P],
+                                        h3[:, c, t, nl * P:(nl + 1) * P], identf[:])
 
         def row_max(c):
             for half in range(2):
@@ -315,11 +314,14 @@ def tile_network_kernel(tc, data, W1, b1, a1, W2, b2, a2, W3, b3, a3, out):
                 l, c, t = units[j]
                 if l < 2 and t == 3:
                     if (l, c) in REG_ACT:
+                        if DVE_COLS > 0:
+                            regroup(l, c, 0, DVE_COLS, False)
+                        w = (CW - DVE_COLS) // REG_PIECES
                         for piece in range(REG_PIECES):
-                            reg_q.append((k + piece, l, c, piece))
+                            reg_q.append((k + piece, l, c, DVE_COLS + piece * w, DVE_COLS + (piece + 1) * w))
                         quant_q.append((k + REG_PIECES + 1, l, c))
                     else:
-                        regroup(l, c, 0, 1)
+                        regroup(l, c, 0, CW, False)
                         quant_q.append((k + 1, l, c))
                 if l == 2 and t == 1:
                     otr_q.append(c)
@@ -331,7 +333,7 @@ def tile_network_kernel(tc, data, W1, b1, a1, W2, b2, a2, W3, b3, a3, out):
                 affine(k - LQ)
             for q in reg_q:
                 if q[0] <= k:
-                    regroup(q[1], q[2], q[3], REG_PIECES)
+                    regroup(q[1], q[2], q[3], q[4], True)
             reg_q = [q for q in reg_q if q[0] > k]
             for c in range(1, NCH):
                 if k == 4 * c - PE_A:

@@ -25,7 +25,7 @@ INV_2PI = 1.0 / (2.0 * math.pi)
 MANUAL = False
 PE_A = 2
 T_A = 1
-DVE_COLS = 128
+DVE_COLS = 0
 LS, LP, LQ, LH = 1, 2, 3, 4
 POOL_Q_MOD = 2
 REG_ACT = ((0, 0), (0, 1), (0, 2), (0, 3), (1, 0), (1, 1), (1, 2))
@@ -54,23 +54,22 @@ def tile_network_kernel(tc, data, W1, b1, a1, W2, b2, a2, W3, b3, a3, out):
         dview = data.rearrange("(p n) k -> p n k", n=16)
         oview = out.rearrange("(p n) c -> p n c", n=16)
 
-        nc.sync.dma_start(out=a1r[:], in_=a1.rearrange("(p t) c -> p t c", t=4))
-        nc.sync.dma_start(out=b1r[:], in_=b1.rearrange("(p t) -> p t", t=4))
         nc.sync.dma_start(out=data_sb[:, 0:4, :], in_=dview[:, 0:4, :])
         nc.sync.dma_start(out=w1r[:], in_=W1.rearrange("(kt q) n -> q kt n", q=P))
+        nc.sync.dma_start(out=a1r[:], in_=a1.rearrange("(p t) c -> p t c", t=4))
+        nc.sync.dma_start(out=b1r[:], in_=b1.rearrange("(p t) -> p t", t=4))
+        nc.sync.dma_start(out=a2r[:], in_=a2.rearrange("(p t) c -> p t c", t=4))
+        nc.sync.dma_start(out=b2r[:], in_=b2.rearrange("(p t) -> p t", t=4))
+        nc.sync.dma_start(out=a3r[:], in_=a3.rearrange("(t p) c -> p t c", p=P))
+        with nc.allow_non_contiguous_dma(reason="256 bias values, one per partition and node tile"):
+            nc.sync.dma_start(out=b3r[:], in_=b3.rearrange("(t p) -> p t", p=P))
+        nc.sync.dma_start(out=data_sb[:, 4:16, :], in_=dview[:, 4:16, :])
         nc.sync.dma_start(out=w2r[:], in_=W2.rearrange("(p j) n -> p j n", j=4))
         nc.sync.dma_start(out=w3r[:], in_=W3.rearrange("(p j) n -> p j n", j=4))
-        nc.sync.dma_start(out=data_sb[:, 4:16, :], in_=dview[:, 4:16, :])
 
         warm = const.tile([P, 1], F32, name="warm")
         nc.vector.memset(warm[:], 0.0)
         nc.scalar.activation(out=warm[:], in_=warm[:], func=ACT.Silu)
-
-        nc.scalar.dma_start(out=a2r[:], in_=a2.rearrange("(p t) c -> p t c", t=4))
-        nc.scalar.dma_start(out=b2r[:], in_=b2.rearrange("(p t) -> p t", t=4))
-        nc.scalar.dma_start(out=a3r[:], in_=a3.rearrange("(t p) c -> p t c", p=P))
-        with nc.allow_non_contiguous_dma(reason="256 bias values, one per partition and node tile"):
-            nc.scalar.dma_start(out=b3r[:], in_=b3.rearrange("(t p) -> p t", p=P))
 
         identb = const.tile([P, P], BF16, name="identb")
         make_identity(nc, identb[:])
@@ -103,16 +102,17 @@ def tile_network_kernel(tc, data, W1, b1, a1, W2, b2, a2, W3, b3, a3, out):
         prep(a3r, b3r, 2, 8)
 
         g2 = const.tile([P, 512, 4], BF16, name="g2", align_bytes=64)
-        nc.gpsimd.tensor_scalar(
-            out=g2.rearrange("p (t m) j -> p t m j", t=4),
-            in0=w2r.rearrange("p j (m t) -> p t m j", t=4),
-            scalar1=1.0, scalar2=0.0, op0=ALU.mult, op1=ALU.add,
-        )
         g3 = const.tile([P, 256, 4], BF16, name="g3", align_bytes=64)
-        nc.gpsimd.tensor_scalar(
-            out=g3[:], in0=w3r.rearrange("p j n -> p n j"),
-            scalar1=1.0, scalar2=0.0, op0=ALU.mult, op1=ALU.add,
-        )
+        w2v = w2r.rearrange("p j (m t) -> p t m j", t=4)
+        w3v = w3r.rearrange("p j n -> p n j")
+
+        def weight_regroup(piece):
+            if piece < 4:
+                nc.scalar.copy(out=g2[:, piece * P:(piece + 1) * P, :], in_=w2v[:, piece, :, :])
+            else:
+                n0 = (piece - 4) * P
+                nc.scalar.copy(out=g3[:, n0:n0 + P, :], in_=w3v[:, n0:n0 + P, :])
+
         w2c = const.tile([P, 512], U32, name="w2c", align_bytes=64)
         w2s = const.tile([P, 512], U8, name="w2s", align_bytes=64)
         w3c = const.tile([P, 256], U32, name="w3c", align_bytes=64)
@@ -302,10 +302,10 @@ def tile_network_kernel(tc, data, W1, b1, a1, W2, b2, a2, W3, b3, a3, out):
                 if q[0] <= k:
                     quantise(q[1], q[2])
             quant_q = [q for q in quant_q if q[0] > k]
-            if k == 5:
+            if k == 7:
                 nc.vector.quantize_mx(out=w2c[:].bitcast(FP8X4), scales=w2s[:],
                                       in_=g2.rearrange("p w j -> p (w j)"))
-            if k == 7:
+            if k == 9:
                 nc.vector.quantize_mx(out=w3c[:].bitcast(FP8X4), scales=w3s[:],
                                       in_=g3.rearrange("p w j -> p (w j)"))
             if 0 <= k < NU:
@@ -335,6 +335,8 @@ def tile_network_kernel(tc, data, W1, b1, a1, W2, b2, a2, W3, b3, a3, out):
                 if q[0] <= k:
                     regroup(q[1], q[2], q[3], q[4], True)
             reg_q = [q for q in reg_q if q[0] > k]
+            if 0 <= k < 6:
+                weight_regroup(k)
             for c in range(1, NCH):
                 if k == 4 * c - PE_A:
                     data_evac(c)

@@ -163,7 +163,10 @@ def tile_network_kernel(tc, data, W1, b1, a1, W2, b2, a2, W3, b3, a3, out):
             st["tp", c] = tp
 
         def data_evac(c):
-            nc.scalar.copy(out=dT[c][:], in_=st["tp", c][:])
+            if c == 0:
+                nc.scalar.copy(out=dT[c][:], in_=st["tp", c][:])
+            else:
+                nc.vector.tensor_copy(out=dT[c][:], in_=st["tp", c][:])
             live[0] -= 1
 
         def pe(u):
@@ -212,7 +215,7 @@ def tile_network_kernel(tc, data, W1, b1, a1, W2, b2, a2, W3, b3, a3, out):
             nc.gpsimd.tensor_tensor(out=tt[:], in0=tt[:], in1=st["f", u][:], op=ALU.mult)
 
         def pool_q(u):
-            return u >= NU - 4 or (u % 4) < POOL_Q_MOD
+            return u >= NU - 4 or (u % 8) in (0, 1, 2, 4, 5)
 
         def affine(u):
             tt = st["t", u]

@@ -163,10 +163,7 @@ def tile_network_kernel(tc, data, W1, b1, a1, W2, b2, a2, W3, b3, a3, out):
             st["tp", c] = tp
 
         def data_evac(c):
-            if c == 0:
-                nc.scalar.copy(out=dT[c][:], in_=st["tp", c][:])
-            else:
-                nc.vector.tensor_copy(out=dT[c][:], in_=st["tp", c][:])
+            nc.scalar.copy(out=dT[c][:], in_=st["tp", c][:])
             live[0] -= 1
 
         def pe(u):
@@ -215,7 +212,7 @@ def tile_network_kernel(tc, data, W1, b1, a1, W2, b2, a2, W3, b3, a3, out):
             nc.gpsimd.tensor_tensor(out=tt[:], in0=tt[:], in1=st["f", u][:], op=ALU.mult)
 
         def pool_q(u):
-            return u >= NU - 4 or (u % 8) in (0, 1, 2, 4, 5)
+            return u >= NU - 4 or (u % 8) in (0, 1, 4)
 
         def affine(u):
             tt = st["t", u]

@@ -212,7 +212,7 @@ def tile_network_kernel(tc, data, W1, b1, a1, W2, b2, a2, W3, b3, a3, out):
             nc.gpsimd.tensor_tensor(out=tt[:], in0=tt[:], in1=st["f", u][:], op=ALU.mult)
 
         def pool_q(u):
-            return u >= NU - 4 or (u % 8) in (0, 1, 4)
+            return u >= NU - 4 or (u % 8) in (0, 1, 2, 4, 5)
 
         def affine(u):
             tt = st["t", u]

from contextlib import ExitStack
import math

import concourse.mybir as mybir
from concourse.masks import make_identity

FLOPS = 2 * 2048 * (256 * 512 + 512 * 512 + 512 * 256)

F32 = mybir.dt.float32
BF16 = mybir.dt.bfloat16
I32 = mybir.dt.int32
U32 = mybir.dt.uint32
U8 = mybir.dt.uint8
FP8X4 = mybir.dt.float8_e4m3fn_x4
ACT = mybir.ActivationFunctionType
ALU = mybir.AluOpType
AX = mybir.AxisListType

P = 128
CW = 512
NCH = 4
TWO_PI = 2.0 * math.pi
INV_2PI = 1.0 / (2.0 * math.pi)

MANUAL = False
PE_A = 2
T_A = 1
DVE_COLS = 0
LS, LP, LQ, LH = 1, 2, 3, 4
POOL_Q_MOD = 2
REG_ACT = ((0, 0), (0, 1), (0, 2), (0, 3), (1, 0), (1, 1), (1, 2))
REG_PIECES = 2


def tile_network_kernel(tc, data, W1, b1, a1, W2, b2, a2, W3, b3, a3, out):
    nc = tc.nc
    with ExitStack() as ctx:
        const = ctx.enter_context(tc.tile_pool(name="const", bufs=1))
        work = ctx.enter_context(tc.tile_pool(name="work", bufs=2))
        psum = ctx.enter_context(tc.psum_pool(name="psum", bufs=8))
        if MANUAL:
            ctx.enter_context(tc.manual_schedule())

        a1r = const.tile([P, 4, 5], BF16, name="a1r")
        b1r = const.tile([P, 4], BF16, name="b1r")
        a2r = const.tile([P, 4, 5], BF16, name="a2r")
        b2r = const.tile([P, 4], BF16, name="b2r")
        a3r = const.tile([P, 2, 5], BF16, name="a3r")
        b3r = const.tile([P, 2], BF16, name="b3r")
        data_sb = const.tile([P, 16, 256], BF16, name="data_sb")
        w1r = const.tile([P, 2, 512], BF16, name="w1r")
        w2r = const.tile([P, 4, 512], BF16, name="w2r")
        w3r = const.tile([P, 4, 256], BF16, name="w3r")
        dview = data.rearrange("(p n) k -> p n k", n=16)
        oview = out.rearrange("(p n) c -> p n c", n=16)

        nc.sync.dma_start(out=data_sb[:, 0:4, :], in_=dview[:, 0:4, :])
        nc.sync.dma_start(out=w1r[:], in_=W1.rearrange("(kt q) n -> q kt n", q=P))
        nc.sync.dma_start(out=a1r[:], in_=a1.rearrange("(p t) c -> p t c", t=4))
        nc.sync.dma_start(out=b1r[:], in_=b1.rearrange("(p t) -> p t", t=4))
        nc.sync.dma_start(out=a2r[:], in_=a2.rearrange("(p t) c -> p t c", t=4))
        nc.sync.dma_start(out=b2r[:], in_=b2.rearrange("(p t) -> p t", t=4))
        nc.sync.dma_start(out=a3r[:], in_=a3.rearrange("(t p) c -> p t c", p=P))
        with nc.allow_non_contiguous_dma(reason="256 bias values, one per partition and node tile"):
            nc.sync.dma_start(out=b3r[:], in_=b3.rearrange("(t p) -> p t", p=P))
        nc.sync.dma_start(out=data_sb[:, 4:16, :], in_=dview[:, 4:16, :])
        nc.sync.dma_start(out=w2r[:], in_=W2.rearrange("(p j) n -> p j n", j=4))
        nc.sync.dma_start(out=w3r[:], in_=W3.rearrange("(p j) n -> p j n", j=4))

        warm = const.tile([P, 1], F32, name="warm")
        nc.vector.memset(warm[:], 0.0)
        nc.scalar.activation(out=warm[:], in_=warm[:], func=ACT.Silu)

        identb = const.tile([P, P], BF16, name="identb")
        make_identity(nc, identb[:])
        identf = const.tile([P, P], F32, name="identf")
        make_identity(nc, identf[:])

        w1p = const.tile([P, 2, 4, P], BF16, name="w1p")
        w1v = w1r.rearrange("q kt (m t) -> q kt t m", t=4)
        for t in range(4):
            nc.vector.tensor_copy(out=w1p[:, :, t, :], in_=w1v[:, :, t, :])

        prm = const.tile([P, 6, 10], F32, name="prm")
        a32s = []

        def prep(ar, br, nt, s0):
            sl = slice(s0, s0 + nt)
            a32 = const.tile([P, nt, 5], F32, name="a32_%d" % s0)
            a32s.append(a32)
            nc.vector.tensor_copy(out=a32[:], in_=ar[:])
            nc.vector.tensor_copy(out=prm[:, 0, sl], in_=br[:])
            nc.vector.tensor_tensor(out=prm[:, 3, sl], in0=a32[:, :, 1], in1=prm[:, 0, sl], op=ALU.mult)
            nc.vector.tensor_tensor(out=prm[:, 3, sl], in0=prm[:, 3, sl], in1=a32[:, :, 2], op=ALU.add)
            nc.vector.tensor_scalar(out=prm[:, 2, sl], in0=prm[:, 3, sl], scalar1=INV_2PI, scalar2=None, op0=ALU.mult)
            nc.vector.tensor_scalar(out=prm[:, 1, sl], in0=a32[:, :, 1], scalar1=INV_2PI, scalar2=None, op0=ALU.mult)
            nc.vector.tensor_tensor(out=prm[:, 5, sl], in0=a32[:, :, 3], in1=prm[:, 0, sl], op=ALU.mult)
            nc.vector.tensor_tensor(out=prm[:, 5, sl], in0=prm[:, 5, sl], in1=a32[:, :, 4], op=ALU.add)

        prep(a1r, b1r, 4, 0)
        prep(a2r, b2r, 4, 4)
        prep(a3r, b3r, 2, 8)

        g2 = const.tile([P, 512, 4], BF16, name="g2", align_bytes=64)
        g3 = const.tile([P, 256, 4], BF16, name="g3", align_bytes=64)
        w2v = w2r.rearrange("p j (m t) -> p t m j", t=4)
        w3v = w3r.rearrange("p j n -> p n j")

        def weight_regroup(piece):
            if piece < 4:
                nc.scalar.copy(out=g2[:, piece * P:(piece + 1) * P, :], in_=w2v[:, piece, :, :])
            else:
                n0 = (piece - 4) * P
                nc.scalar.copy(out=g3[:, n0:n0 + P, :], in_=w3v[:, n0:n0 + P, :])

        w2c = const.tile([P, 512], U32, name="w2c", align_bytes=64)
        w2s = const.tile([P, 512], U8, name="w2s", align_bytes=64)
        w3c = const.tile([P, 256], U32, name="w3c", align_bytes=64)
        w3s = const.tile([P, 256], U8, name="w3s", align_bytes=64)

        hc = [const.tile([P, NCH, CW], U32, name="hc%d" % l, align_bytes=64) for l in range(2)]
        hs = [const.tile([P, NCH, CW], U8, name="hs%d" % l, align_bytes=64) for l in range(2)]
        h3 = const.tile([P, NCH, 2, CW], F32, name="h3")
        dT = [const.tile([P, 2, CW], BF16, name="dT%d" % c) for c in range(NCH)]
        ex = const.tile([P, 16, 256], F32, name="ex")
        nmx = const.tile([P, 16], F32, name="nmx")
        ssum = const.tile([P, 16], F32, name="ssum")
        rs = const.tile([P, 16], F32, name="rs")

        units = []
        for c in range(NCH):
            for t in range(4):
                units.append((0, c, t))
        for c in range(NCH):
            for t in range(4):
                units.append((1, c, t))
        for c in range(NCH):
            for t in range(2):
                units.append((2, c, t))
        NU = len(units)
        st = {}
        live = [0]

        def par(row, u):
            l, c, t = units[u]
            s = 4 * l + t
            return prm[:, row, s:s + 1]

        def apar(col, u):
            l, c, t = units[u]
            return a32s[l][:, t, col:col + 1]

        def data_transposes(c):
            tp = psum.tile([P, 2, CW], BF16, name="tp", tag="bank")
            live[0] += 1
            for kt in range(2):
                for nl in range(4):
                    nc.tensor.transpose(
                        tp[:, kt, nl * P:(nl + 1) * P],
                        data_sb[:, 4 * c + nl, kt * P:(kt + 1) * P],
                        identb[:],
                    )
            st["tp", c] = tp

        def data_evac(c):
            nc.scalar.copy(out=dT[c][:], in_=st["tp", c][:])
            live[0] -= 1

        def pe(u):
            l, c, t = units[u]
            z = psum.tile([P, CW], F32, name="z", tag="bank")
            st["z", u] = z
            live[0] += 1
            if l == 0:
                for kt in range(2):
                    nc.tensor.matmul(out=z[:], lhsT=w1p[:, kt, t, :], rhs=dT[c][:, kt, :],
                                     start=(kt == 0), stop=(kt == 1))
            else:
                wc, ws = (w2c, w2s) if l == 1 else (w3c, w3s)
                nc.tensor.matmul_mx(
                    out=z[:],
                    lhsT=wc[:, t * P:(t + 1) * P].bitcast(FP8X4),
                    lhsT_scale=ws[:, t * P:(t + 1) * P],
                    rhs=hc[l - 1][:, c, :].bitcast(FP8X4),
                    rhs_scale=hs[l - 1][:, c, :],
                    start=True, stop=True,
                )

        def tanh(u):
            tt = work.tile([P, CW], F32, name="tt", tag="tt", bufs=8)
            st["t", u] = tt
            nc.scalar.activation(out=tt[:], in_=st["z", u][:], func=ACT.Tanh, bias=par(0, u), scale=1.0)

        def round_arg(u):
            nn = work.tile([P, CW], I32, name="nn", tag="nn", bufs=2)
            st["n", u] = nn
            nc.vector.tensor_scalar(out=nn[:], in0=st["z", u][:], scalar1=par(1, u), scalar2=par(2, u),
                                    op0=ALU.mult, op1=ALU.add)

        def frac_arg(u):
            ff = work.tile([P, CW], F32, name="ff", tag="ff", bufs=4)
            st["f", u] = ff
            nc.vector.scalar_tensor_tensor(out=ff[:], in0=st["z", u][:], scalar=par(1, u), in1=st["n", u][:],
                                           op0=ALU.mult, op1=ALU.subtract)

        def sin(u):
            ff = st["f", u]
            nc.scalar.activation(out=ff[:], in_=ff[:], func=ACT.Sin, bias=par(3, u), scale=TWO_PI)

        def prod(u):
            tt = st["t", u]
            nc.gpsimd.tensor_tensor(out=tt[:], in0=tt[:], in1=st["f", u][:], op=ALU.mult)

        def pool_q(u):
            return u >= NU - 4 or (u % 8) in (0, 1, 2, 4, 5)

        def affine(u):
            tt = st["t", u]
            if pool_q(u):
                nc.gpsimd.tensor_scalar(out=tt[:], in0=tt[:], scalar1=apar(0, u), scalar2=par(5, u),
                                        op0=ALU.mult, op1=ALU.add)
            else:
                nc.scalar.activation(out=tt[:], in_=tt[:], func=ACT.Identity, bias=par(5, u), scale=apar(0, u))

        def combine(u):
            l, c, t = units[u]
            if l < 2:
                if t == 0:
                    st["h", l, c] = work.tile([P, 4, CW], BF16, name="hh", tag="hh", bufs=3)
                dst = st["h", l, c][:, t, :]
            else:
                dst = h3[:, c, t, :]
            nc.vector.scalar_tensor_tensor(out=dst, in0=st["z", u][:], scalar=apar(3, u), in1=st["t", u][:],
                                           op0=ALU.mult, op1=ALU.add)
            live[0] -= 1

        def regroup(l, c, w0, w1, on_scalar):
            if w0 == 0:
                st["g", l, c] = work.tile([P, CW, 4], BF16, name="gg", tag="gg", bufs=3, align_bytes=64)
            dst = st["g", l, c][:, w0:w1, :].rearrange("p (c i) t -> p c t i", i=4)
            src = st["h", l, c][:, :, w0:w1].rearrange("p t (c i) -> p c t i", i=4)
            if on_scalar:
                nc.scalar.copy(out=dst, in_=src)
            else:
                nc.vector.tensor_copy(out=dst, in_=src)

        def quantise(l, c):
            nc.vector.quantize_mx(
                out=hc[l][:, c, :].bitcast(FP8X4),
                scales=hs[l][:, c, :],
                in_=st["g", l, c].rearrange("p w t -> p (w t)"),
            )

        def out_transposes(c):
            for half in range(2):
                st["o", c, half] = psum.tile([P, 2, 256], F32, name="ot", tag="bank")
                live[0] += 1
            for t in range(2):
                for nl in range(4):
                    nc.tensor.transpose(st["o", c, nl // 2][:, nl % 2, t * P:(t + 1) * P],
                                        h3[:, c, t, nl * P:(nl + 1) * P], identf[:])

        def row_max(c):
            for half in range(2):
                n0 = 4 * c + 2 * half
                nc.vector.tensor_reduce(out=nmx[:, n0:n0 + 2], in_=st["o", c, half][:], axis=AX.X, op=ALU.max,
                                        negate=True)

        def exps(c):
            for half in range(2):
                for j in range(2):
                    n = 4 * c + 2 * half + j
                    nc.scalar.activation(out=ex[:, n, :], in_=st["o", c, half][:, j, :], func=ACT.Exp,
                                         bias=nmx[:, n:n + 1], scale=1.0, accum_out=ssum[:, n:n + 1])
                live[0] -= 1

        def normalise(c):
            nc.vector.reciprocal(out=rs[:, 4 * c:4 * c + 4], in_=ssum[:, 4 * c:4 * c + 4])
            for n in range(4 * c, 4 * c + 4):
                nc.vector.tensor_scalar(out=ex[:, n, :], in0=ex[:, n, :], scalar1=rs[:, n:n + 1], scalar2=None,
                                        op0=ALU.mult)
            nc.sync.dma_start(out=oview[:, 4 * c:4 * c + 4, :], in_=ex[:, 4 * c:4 * c + 4, :])

        data_transposes(0)
        data_evac(0)
        quant_q = []
        reg_q = []
        otr_q = []
        max_q = []
        exp_q = []
        for k in range(-PE_A, NU + LH):
            if 0 <= k + T_A < NU:
                tanh(k + T_A)
            if 0 <= k - LS < NU:
                sin(k - LS)
            if 0 <= k < NU:
                round_arg(k)
            j = k - LH
            if 0 <= j < NU:
                combine(j)
            for q in quant_q:
                if q[0] <= k:
                    quantise(q[1], q[2])
            quant_q = [q for q in quant_q if q[0] > k]
            if k == 7:
                nc.vector.quantize_mx(out=w2c[:].bitcast(FP8X4), scales=w2s[:],
                                      in_=g2.rearrange("p w j -> p (w j)"))
            if k == 9:
                nc.vector.quantize_mx(out=w3c[:].bitcast(FP8X4), scales=w3s[:],
                                      in_=g3.rearrange("p w j -> p (w j)"))
            if 0 <= k < NU:
                frac_arg(k)
            if 0 <= j < NU:
                l, c, t = units[j]
                if l < 2 and t == 3:
                    if (l, c) in REG_ACT:
                        if DVE_COLS > 0:
                            regroup(l, c, 0, DVE_COLS, False)
                        w = (CW - DVE_COLS) // REG_PIECES
                        for piece in range(REG_PIECES):
                            reg_q.append((k + piece, l, c, DVE_COLS + piece * w, DVE_COLS + (piece + 1) * w))
                        quant_q.append((k + REG_PIECES + 1, l, c))
                    else:
                        regroup(l, c, 0, CW, False)
                        quant_q.append((k + 1, l, c))
                if l == 2 and t == 1:
                    otr_q.append(c)
            if 0 <= k - LP < NU:
                prod(k - LP)
                if pool_q(k - LP):
                    affine(k - LP)
            if 0 <= k - LQ < NU and not pool_q(k - LQ):
                affine(k - LQ)
            for q in reg_q:
                if q[0] <= k:
                    regroup(q[1], q[2], q[3], q[4], True)
            reg_q = [q for q in reg_q if q[0] > k]
            if 0 <= k < 6:
                weight_regroup(k)
            for c in range(1, NCH):
                if k == 4 * c - PE_A:
                    data_evac(c)
            for c in range(1, NCH):
                if k == 4 * c - PE_A - 1:
                    data_transposes(c)
            if 0 <= k + PE_A < NU:
                pe(k + PE_A)
            if len(otr_q) > 0 and live[0] <= 6 and k < NU + LH - 1:
                out_transposes(otr_q[0])
                max_q.append(otr_q[0])
                otr_q = otr_q[1:]
            if k >= NU - 1 and len(max_q) > 0:
                row_max(max_q[0])
                exp_q.append(max_q[0])
                max_q = max_q[1:]
            if k - LS >= NU - 1:
                for c in exp_q:
                    exps(c)
                exp_q = []

        normalise(0)
        out_transposes(3)
        row_max(3)
        exps(3)
        normalise(1)
        normalise(2)
        normalise(3)
